import numpy as np
import ml_dtypes


def mxq(x, axis, fmt="e4m3"):
    dtype, down = {"e4m3": (ml_dtypes.float8_e4m3fn, 7), "e5m2": (ml_dtypes.float8_e5m2, 14)}[fmt]
    v = np.moveaxis(np.asarray(x, np.float32).astype(ml_dtypes.bfloat16).astype(np.float64), axis, -1)
    blocks = v.reshape(v.shape[:-1] + (-1, 32))
    amax = np.abs(blocks).max(-1, keepdims=True)
    byte = np.maximum(np.where(amax > 0, np.frexp(amax)[1] - 1 + 127, 0) - down, 1)
    scale = np.exp2(byte - 127.0)
    codes = (blocks / scale).astype(np.float32).astype(dtype).astype(np.float64)
    return np.moveaxis((codes * scale).reshape(v.shape), -1, axis)


WIDE = False


def mx_kscale(k):
    if not WIDE:
        return np.ones(k)
    levels = np.array([10, -10, 5, -5, 0])
    a = np.random.permutation(np.resize(levels, k // 512 * 4)).reshape(k // 512, 4)
    idx = np.arange(k)
    return np.exp2(a[idx // 512, idx % 128 // 32])


BF16 = ml_dtypes.bfloat16


def bf(x):
    return np.asarray(x, np.float32).astype(BF16)


def f64(x):
    return np.asarray(x).astype(np.float64)


E2M1 = np.array([0.0, 0.5, 1.0, 1.5, 2.0, 3.0, 4.0, 6.0, -0.0, -0.5, -1.0, -1.5, -2.0, -3.0, -4.0, -6.0])


def pack_weight(w, fmt):
    k, n = w.shape
    w = f64(bf(w)).reshape(k // 32, 32, n)
    amax = np.abs(w).max(1)
    if fmt == "e4m3":
        byte = np.frexp(amax)[1] - 1 + 127 - 7
    else:
        mant, ex = np.frexp(amax / 6.0)
        byte = np.where(mant > 0.5, ex, ex - 1) + 127
    byte = np.clip(np.where(amax > 0, byte, 1), 1, 254)
    scaled = (w * np.exp2(127.0 - byte)[:, None, :]).reshape(k, n).astype(np.float32)
    by_word = np.ascontiguousarray(scaled.reshape(k // 512, 128, 4, n).transpose(0, 1, 3, 2))
    if fmt == "e4m3":
        words = by_word.astype(ml_dtypes.float8_e4m3fn).view(np.uint8)
    else:
        c = by_word.astype(ml_dtypes.float4_e2m1fn).view(np.uint8) & 0xF
        words = c[..., 0::2] | (c[..., 1::2] << 4)
    return np.ascontiguousarray(words), np.ascontiguousarray(byte.astype(np.uint8).reshape(k // 512, 16, n))


def unpack_weight(words, scales, fmt):
    g, p, n, _ = words.shape
    if fmt == "e4m3":
        vals = np.ascontiguousarray(words).view(ml_dtypes.float8_e4m3fn).astype(np.float64)
    else:
        nib = np.empty((g, p, n, 4), np.uint8)
        nib[..., 0::2] = words & 0xF
        nib[..., 1::2] = words >> 4
        vals = E2M1[nib]
    vals = vals * np.repeat(np.exp2(scales.astype(np.float64) - 127.0), 8, axis=1)[..., None]
    return vals.transpose(0, 1, 3, 2).reshape(g * 512, n)

def pack4(w):
    words, scales = pack_weight(w, "e2m1")
    return words.reshape(words.shape[0], 128, -1), scales


def unpack4(words, scales):
    return unpack_weight(words.reshape(words.shape[0], 128, -1, 2), scales, "e2m1")


N, S, D, H, O = 4, 64, 16384, 512, 1024


def elu(v):
    return np.where(v > 0.0, v, np.exp(np.minimum(v, 0.0)) - 1.0)


def setup_inputs():
    s = mx_kscale(D)
    x = bf(np.random.standard_normal((N, S, D)) * s)
    Wk_words, Wk_scales = pack4(np.random.standard_normal((D, H)) / np.sqrt(D) / s[:, None])
    bk = bf(np.random.standard_normal(H) * 0.1)
    Wv_words, Wv_scales = pack4(np.random.standard_normal((D, H)) / np.sqrt(D) / s[:, None])
    bv = bf(np.random.standard_normal(H) * 0.1)
    return {"x": x,
            "Wk_words": Wk_words,
            "Wk_scales": Wk_scales,
            "bk": bk,
            "Wv_words": Wv_words,
            "Wv_scales": Wv_scales,
            "bv": bv}


def reference(x, Wk_words, Wk_scales, bk, Wv_words, Wv_scales, bv):
    xq = mxq(f64(x), 2, "e4m3")
    keyp = (xq @ unpack4(Wk_words, Wk_scales)) + f64(bk)
    value = (xq @ unpack4(Wv_words, Wv_scales)) + f64(bv)
    K = elu(keyp) + 1.0
    KV = np.sum(K * value, axis=1)
    Ksum = np.sum(K, axis=1)
    return KV, Ksum

@@ -1,0 +1,205 @@
+from contextlib import ExitStack
+
+import concourse.mybir as mybir
+from concourse.masks import make_identity
+
+F32 = mybir.dt.float32
+BF16 = mybir.dt.bfloat16
+I32 = mybir.dt.int32
+U32 = mybir.dt.uint32
+U8 = mybir.dt.uint8
+FP8X4 = mybir.dt.float8_e4m3fn_x4
+FP4X4 = mybir.dt.float4_e2m1fn_x4
+ACT = mybir.ActivationFunctionType
+ALU = mybir.AluOpType
+
+P = 128
+BATCH, SEQ, D, H = 4, 64, 16384, 512
+ROWS = BATCH * SEQ
+ROW_TILES = ROWS // P
+K_PASS = 4 * P
+GROUPS = D // K_PASS
+HALVES = 2
+BUNCH = 4
+BUNCHES = GROUPS // BUNCH
+SCALE_RUN = GROUPS // 2
+SCALE_CUT = 8
+
+FLOPS = 2 * ROWS * D * 2 * H
+
+
+def tile_linearattention_pa_k_kernel(
+    tc, x, Wk_words, Wk_scales, bk, Wv_words, Wv_scales, bv, out_0, out_1
+):
+    nc = tc.nc
+    x_rows = x.rearrange("n s d -> (n s) d")
+
+    with ExitStack() as ctx:
+        keep = ctx.enter_context(tc.tile_pool(name="keep", bufs=1))
+        x_pool = ctx.enter_context(tc.tile_pool(name="x_pool", bufs=4))
+        grouped_pool = ctx.enter_context(tc.tile_pool(name="grouped_pool", bufs=2))
+        sums = ctx.enter_context(tc.psum_pool(name="sums", bufs=1))
+        banks = ctx.enter_context(tc.psum_pool(name="banks", bufs=4))
+        ctx.enter_context(tc.manual_schedule())
+
+        words = {}
+        planes = {}
+        for w in ("k", "v"):
+            words[w] = keep.tile([P, GROUPS, 2 * H], U8, name="words_%s" % w, align_bytes=64)
+            planes[w] = keep.tile([P, GROUPS, H], U8, name="planes_%s" % w, align_bytes=64)
+        x_codes = keep.tile([P, GROUPS, ROW_TILES, P], U32, name="x_codes", align_bytes=64)
+        x_planes = keep.tile([P, GROUPS, ROW_TILES, P], U8, name="x_planes", align_bytes=64)
+        ident = keep.tile([P, P], F32, name="ident")
+        ones = keep.tile([P, P], BF16, name="ones")
+        bias_row = keep.tile([P, 2, H], BF16, name="bias_row")
+        bias_all = keep.tile([P, 2, H], F32, name="bias_all")
+        batch_of_row = keep.tile([P, ROW_TILES, P], F32, name="batch_of_row")
+
+        acc = {}
+        for w in ("k", "v"):
+            for m in range(ROW_TILES):
+                acc[(w, m)] = sums.tile([P, H], F32, name="acc_%s%d" % (w, m))
+
+        make_identity(nc, ident[:])
+        nc.vector.memset(bias_row[:].bitcast(I32), 0)
+        nc.vector.memset(ones[:], 1.0)
+        nc.vector.memset(batch_of_row[:], 0.0)
+        for m in range(ROW_TILES):
+            for half in range(P // SEQ):
+                c = m * (P // SEQ) + half
+                nc.vector.memset(batch_of_row[half * SEQ : (half + 1) * SEQ, m, c : c + 1], 1.0)
+        for w in ("k", "v"):
+            for run in range(GROUPS // SCALE_RUN):
+                g0 = run * SCALE_RUN
+                nc.vector.memset(planes[w][:, g0 : g0 + SCALE_RUN, :].bitcast(I32), 0)
+
+        x_tiles = {}
+
+        def load_x(b):
+            cols = slice(b * BUNCH * K_PASS, (b + 1) * BUNCH * K_PASS)
+            x_tiles[b] = x_pool.tile([P, ROW_TILES, BUNCH * K_PASS], BF16, name="x_raw")
+            nc.sync.dma_start(
+                out=x_tiles[b][:], in_=x_rows[:, cols].rearrange("(m p) c -> p m c", p=P)
+            )
+
+        def load_words(w, dram, b):
+            g0 = b * BUNCH
+            nc.sync.dma_start(
+                out=words[w][:, g0 : g0 + BUNCH, :].bitcast(I32),
+                in_=dram[g0 : g0 + BUNCH].rearrange("g p c -> p g c").bitcast(I32),
+            )
+
+        def load_scales(w, dram, run):
+            by_row = dram.rearrange("g q n -> q g n")
+            for g0 in range(run * SCALE_RUN, (run + 1) * SCALE_RUN, SCALE_CUT):
+                for q in range(8):
+                    part = 32 * (q // 4) + q % 4
+                    nc.sync.dma_start(
+                        out=planes[w][part : P : 64, g0 : g0 + SCALE_CUT, :].bitcast(I32),
+                        in_=by_row[q : 16 : 8, g0 : g0 + SCALE_CUT, :].bitcast(I32),
+                    )
+
+        def load_weight(w, words_dram, scales_dram, b):
+            if (b * BUNCH) % SCALE_RUN == 0:
+                load_scales(w, scales_dram, (b * BUNCH) // SCALE_RUN)
+            load_words(w, words_dram, b)
+
+        def transpose_and_quantise(b):
+            x_words = x_tiles[b][:].bitcast(F32)
+            grouped = grouped_pool.tile(
+                [P, BUNCH, ROW_TILES, P, HALVES], F32, name="grouped", align_bytes=64
+            )
+            for i in range(BUNCH):
+                xt = banks.tile([P, ROW_TILES, HALVES, P], F32, name="xt", tag="bank")
+                for m in range(ROW_TILES):
+                    for u in range(HALVES):
+                        nc.tensor.transpose(
+                            out=xt[:, m, u, :],
+                            in_=x_words[:, m, 256 * i + u : 256 * (i + 1) : HALVES],
+                            identity=ident[:],
+                        )
+                if i % 2 == 0:
+                    nc.scalar.copy(out=grouped[:, i], in_=xt[:].rearrange("p m u r -> p m r u"))
+                else:
+                    nc.vector.tensor_copy(
+                        out=grouped[:, i], in_=xt[:].rearrange("p m u r -> p m r u")
+                    )
+            for i in range(0, BUNCH, 2):
+                g = b * BUNCH + i
+                nc.vector.quantize_mx(
+                    out=x_codes[:, g : g + 2].rearrange("p g m r -> p (g m r)").bitcast(FP8X4),
+                    scales=x_planes[:, g : g + 2].rearrange("p g m r -> p (g m r)"),
+                    in_=grouped[:, i : i + 2].rearrange("p g m r u -> p (g m r u)").bitcast(BF16),
+                )
+
+        def multiply(w, b):
+            for g in range(b * BUNCH, (b + 1) * BUNCH):
+                for m in range(ROW_TILES):
+                    nc.tensor.matmul_mx(
+                        out=acc[(w, m)][:],
+                        lhsT=x_codes[:, g, m, :].bitcast(FP8X4),
+                        lhsT_scale=x_planes[:, g, m, :],
+                        rhs=words[w][:, g, :].bitcast(FP4X4),
+                        rhs_scale=planes[w][:, g, :],
+                        start=(g == 0),
+                        stop=(g == GROUPS - 1),
+                    )
+
+        load_x(0)
+        load_x(1)
+        nc.sync.dma_start(out=bias_row[0:1, 0, :], in_=bk.unsqueeze(0))
+        nc.sync.dma_start(out=bias_row[0:1, 1, :], in_=bv.unsqueeze(0))
+        for b in range(BUNCHES):
+            load_weight("k", Wk_words, Wk_scales, b)
+            if b + 2 < BUNCHES:
+                load_x(b + 2)
+            transpose_and_quantise(b)
+            if b > 0:
+                multiply("k", b - 1)
+        for b in range(BUNCHES):
+            load_weight("v", Wv_words, Wv_scales, b)
+        multiply("k", BUNCHES - 1)
+
+        for j in range(2):
+            spread = banks.tile([P, H], F32, name="spread", tag="bank")
+            nc.tensor.matmul(out=spread[:], lhsT=ones[:], rhs=bias_row[:, j, :], start=True, stop=True)
+            nc.scalar.copy(out=bias_all[:, j, :], in_=spread[:])
+
+        feat = {}
+        for m in range(ROW_TILES):
+            keyp = keep.tile([P, H], F32, name="keyp%d" % m)
+            nc.vector.tensor_tensor(out=keyp[:], in0=acc[("k", m)][:], in1=bias_all[:, 0, :], op=ALU.add)
+            below = keep.tile([P, H], F32, name="below%d" % m)
+            nc.vector.tensor_scalar_min(out=below[:], in0=keyp[:], scalar1=0.0)
+            nc.scalar.activation(out=below[:], in_=below[:], func=ACT.Exp)
+            feat[m] = keep.tile([P, H], F32, name="feat%d" % m)
+            nc.vector.scalar_tensor_tensor(
+                out=feat[m][:], in0=keyp[:], scalar=0.0, in1=below[:], op0=ALU.max, op1=ALU.add
+            )
+
+        ksum = keep.tile([P, H], F32, name="ksum")
+        bias_part = keep.tile([P, H], F32, name="bias_part")
+        for b in range(BUNCHES):
+            multiply("v", b)
+            if b == BUNCHES // 2:
+                ksum_ps = banks.tile([P, H], F32, name="ksum_ps", tag="bank")
+                for m in range(ROW_TILES):
+                    nc.tensor.matmul(
+                        out=ksum_ps[:], lhsT=batch_of_row[:, m, :], rhs=feat[m][:],
+                        start=(m == 0), stop=(m == ROW_TILES - 1),
+                    )
+                nc.vector.tensor_copy(out=ksum[:], in_=ksum_ps[:])
+                nc.vector.tensor_tensor(out=bias_part[:], in0=ksum[:], in1=bias_all[:, 1, :], op=ALU.mult)
+                nc.sync.dma_start(out=out_1, in_=ksum[0:BATCH, :])
+
+        kv_ps = banks.tile([P, H], F32, name="kv_ps", tag="bank")
+        for m in range(ROW_TILES):
+            prod = keep.tile([P, H], F32, name="prod%d" % m)
+            nc.vector.tensor_tensor(out=prod[:], in0=acc[("v", m)][:], in1=feat[m][:], op=ALU.mult)
+            nc.tensor.matmul(
+                out=kv_ps[:], lhsT=batch_of_row[:, m, :], rhs=prod[:],
+                start=(m == 0), stop=(m == ROW_TILES - 1),
+            )
+        kv = keep.tile([P, H], F32, name="kv")
+        nc.vector.tensor_tensor(out=kv[:], in0=kv_ps[:], in1=bias_part[:], op=ALU.add)
+        nc.sync.dma_start(out=out_0, in_=kv[0:BATCH, :])

@@ -23,7 +23,6 @@ HALVES = 2
 BUNCH = 4
 BUNCHES = GROUPS // BUNCH
 SCALE_RUN = GROUPS // 2
-SCALE_CUT = 8
 
 FLOPS = 2 * ROWS * D * 2 * H
 
@@ -68,10 +67,15 @@ def tile_linearattention_pa_k_kernel(
             for half in range(P // SEQ):
                 c = m * (P // SEQ) + half
                 nc.vector.memset(batch_of_row[half * SEQ : (half + 1) * SEQ, m, c : c + 1], 1.0)
-        for w in ("k", "v"):
-            for run in range(GROUPS // SCALE_RUN):
-                g0 = run * SCALE_RUN
+        for w, dram in (("k", Wk_scales), ("v", Wv_scales)):
+            by_row = dram.rearrange("g q n -> q g n")
+            for g0 in range(0, GROUPS, SCALE_RUN):
                 nc.vector.memset(planes[w][:, g0 : g0 + SCALE_RUN, :].bitcast(I32), 0)
+                for r in range(4):
+                    nc.gpsimd.dma_start(
+                        out=planes[w][r : P : 32, g0 : g0 + SCALE_RUN, :].bitcast(F32),
+                        in_=by_row[r : 16 : 4, g0 : g0 + SCALE_RUN, :].bitcast(F32),
+                    )
 
         x_tiles = {}
 
@@ -88,21 +92,6 @@ def tile_linearattention_pa_k_kernel(
                 out=words[w][:, g0 : g0 + BUNCH, :].bitcast(I32),
                 in_=dram[g0 : g0 + BUNCH].rearrange("g p c -> p g c").bitcast(I32),
             )
-
-        def load_scales(w, dram, run):
-            by_row = dram.rearrange("g q n -> q g n")
-            for g0 in range(run * SCALE_RUN, (run + 1) * SCALE_RUN, SCALE_CUT):
-                for q in range(8):
-                    part = 32 * (q // 4) + q % 4
-                    nc.sync.dma_start(
-                        out=planes[w][part : P : 64, g0 : g0 + SCALE_CUT, :].bitcast(I32),
-                        in_=by_row[q : 16 : 8, g0 : g0 + SCALE_CUT, :].bitcast(I32),
-                    )
-
-        def load_weight(w, words_dram, scales_dram, b):
-            if (b * BUNCH) % SCALE_RUN == 0:
-                load_scales(w, scales_dram, (b * BUNCH) // SCALE_RUN)
-            load_words(w, words_dram, b)
 
         def transpose_and_quantise(b):
             x_words = x_tiles[b][:].bitcast(F32)
@@ -150,14 +139,14 @@ def tile_linearattention_pa_k_kernel(
         nc.sync.dma_start(out=bias_row[0:1, 0, :], in_=bk.unsqueeze(0))
         nc.sync.dma_start(out=bias_row[0:1, 1, :], in_=bv.unsqueeze(0))
         for b in range(BUNCHES):
-            load_weight("k", Wk_words, Wk_scales, b)
+            load_words("k", Wk_words, b)
             if b + 2 < BUNCHES:
                 load_x(b + 2)
             transpose_and_quantise(b)
             if b > 0:
                 multiply("k", b - 1)
         for b in range(BUNCHES):
-            load_weight("v", Wv_words, Wv_scales, b)
+            load_words("v", Wv_words, b)
         multiply("k", BUNCHES - 1)
 
         for j in range(2):

@@ -22,6 +22,7 @@ GROUPS = D // K_PASS
 HALVES = 2
 BUNCH = 4
 BUNCHES = GROUPS // BUNCH
+PER_BANK = 2
 SCALE_RUN = GROUPS // 2
 
 FLOPS = 2 * ROWS * D * 2 * H
@@ -32,22 +33,37 @@ def tile_linearattention_pa_k_kernel(
 ):
     nc = tc.nc
     x_rows = x.rearrange("n s d -> (n s) d")
+    words_dram = {"k": Wk_words, "v": Wv_words}
+    scales_dram = {"k": Wk_scales, "v": Wv_scales}
 
     with ExitStack() as ctx:
         keep = ctx.enter_context(tc.tile_pool(name="keep", bufs=1))
-        x_pool = ctx.enter_context(tc.tile_pool(name="x_pool", bufs=4))
-        grouped_pool = ctx.enter_context(tc.tile_pool(name="grouped_pool", bufs=2))
+        x_pool = ctx.enter_context(tc.tile_pool(name="x_pool", bufs=6))
+        sorted_pool = ctx.enter_context(tc.tile_pool(name="sorted_pool", bufs=4))
+        grouped_pool = ctx.enter_context(tc.tile_pool(name="grouped_pool", bufs=4))
         sums = ctx.enter_context(tc.psum_pool(name="sums", bufs=1))
         banks = ctx.enter_context(tc.psum_pool(name="banks", bufs=4))
         ctx.enter_context(tc.manual_schedule())
 
         words = {}
-        planes = {}
         for w in ("k", "v"):
-            words[w] = keep.tile([P, GROUPS, 2 * H], U8, name="words_%s" % w, align_bytes=64)
-            planes[w] = keep.tile([P, GROUPS, H], U8, name="planes_%s" % w, align_bytes=64)
-        x_codes = keep.tile([P, GROUPS, ROW_TILES, P], U32, name="x_codes", align_bytes=64)
-        x_planes = keep.tile([P, GROUPS, ROW_TILES, P], U8, name="x_planes", align_bytes=64)
+            for b in range(BUNCHES):
+                words[(w, b)] = keep.tile(
+                    [P, BUNCH, 2 * H], U8, name="words_%s%d" % (w, b), align_bytes=64
+                )
+        planes = {}
+        for run in range(GROUPS // SCALE_RUN):
+            planes[run] = keep.tile([P, SCALE_RUN, H], U8, name="planes%d" % run, align_bytes=64)
+        x_codes = {}
+        x_planes = {}
+        for b in range(BUNCHES):
+            for m in range(ROW_TILES):
+                x_codes[(b, m)] = keep.tile(
+                    [P, BUNCH, P], U32, name="x_codes%d_%d" % (b, m), align_bytes=64
+                )
+                x_planes[(b, m)] = keep.tile(
+                    [P, BUNCH, P], U8, name="x_planes%d_%d" % (b, m), align_bytes=64
+                )
         ident = keep.tile([P, P], F32, name="ident")
         ones = keep.tile([P, P], BF16, name="ones")
         bias_row = keep.tile([P, 2, H], BF16, name="bias_row")
@@ -60,6 +76,8 @@ def tile_linearattention_pa_k_kernel(
                 acc[(w, m)] = sums.tile([P, H], F32, name="acc_%s%d" % (w, m))
 
         make_identity(nc, ident[:])
+        for run in range(GROUPS // SCALE_RUN):
+            nc.vector.memset(planes[run][:].bitcast(I32), 0)
         nc.vector.memset(bias_row[:].bitcast(I32), 0)
         nc.vector.memset(ones[:], 1.0)
         nc.vector.memset(batch_of_row[:], 0.0)
@@ -67,69 +85,76 @@ def tile_linearattention_pa_k_kernel(
             for half in range(P // SEQ):
                 c = m * (P // SEQ) + half
                 nc.vector.memset(batch_of_row[half * SEQ : (half + 1) * SEQ, m, c : c + 1], 1.0)
-        for w, dram in (("k", Wk_scales), ("v", Wv_scales)):
-            by_row = dram.rearrange("g q n -> q g n")
-            for g0 in range(0, GROUPS, SCALE_RUN):
-                nc.vector.memset(planes[w][:, g0 : g0 + SCALE_RUN, :].bitcast(I32), 0)
-                for r in range(4):
-                    nc.gpsimd.dma_start(
-                        out=planes[w][r : P : 32, g0 : g0 + SCALE_RUN, :].bitcast(F32),
-                        in_=by_row[r : 16 : 4, g0 : g0 + SCALE_RUN, :].bitcast(F32),
-                    )
 
-        x_tiles = {}
+        x_raw = {}
+        x_sorted = {}
+        grouped = {}
 
         def load_x(b):
             cols = slice(b * BUNCH * K_PASS, (b + 1) * BUNCH * K_PASS)
-            x_tiles[b] = x_pool.tile([P, ROW_TILES, BUNCH * K_PASS], BF16, name="x_raw")
-            nc.sync.dma_start(
-                out=x_tiles[b][:], in_=x_rows[:, cols].rearrange("(m p) c -> p m c", p=P)
-            )
+            for m in range(ROW_TILES):
+                x_raw[(b, m)] = x_pool.tile([P, BUNCH * K_PASS], BF16, name="x_raw")
+                nc.sync.dma_start(out=x_raw[(b, m)][:], in_=x_rows[m * P : (m + 1) * P, cols])
 
-        def load_words(w, dram, b):
+        def load_weight(w, b):
             g0 = b * BUNCH
+            if g0 % SCALE_RUN == 0:
+                by_row = scales_dram[w].rearrange("g q n -> q g n")
+                for r in range(4):
+                    nc.sync.dma_start(
+                        out=planes[g0 // SCALE_RUN][r : P : 32, :, :].bitcast(I32),
+                        in_=by_row[r : 16 : 4, g0 : g0 + SCALE_RUN, :].bitcast(I32),
+                    )
             nc.sync.dma_start(
-                out=words[w][:, g0 : g0 + BUNCH, :].bitcast(I32),
-                in_=dram[g0 : g0 + BUNCH].rearrange("g p c -> p g c").bitcast(I32),
+                out=words[(w, b)][:].bitcast(I32),
+                in_=words_dram[w][g0 : g0 + BUNCH].rearrange("g p c -> p g c").bitcast(I32),
             )
 
-        def transpose_and_quantise(b):
-            x_words = x_tiles[b][:].bitcast(F32)
-            grouped = grouped_pool.tile(
-                [P, BUNCH, ROW_TILES, P, HALVES], F32, name="grouped", align_bytes=64
-            )
-            for i in range(BUNCH):
-                xt = banks.tile([P, ROW_TILES, HALVES, P], F32, name="xt", tag="bank")
-                for m in range(ROW_TILES):
-                    for u in range(HALVES):
-                        nc.tensor.transpose(
-                            out=xt[:, m, u, :],
-                            in_=x_words[:, m, 256 * i + u : 256 * (i + 1) : HALVES],
-                            identity=ident[:],
-                        )
-                if i % 2 == 0:
-                    nc.scalar.copy(out=grouped[:, i], in_=xt[:].rearrange("p m u r -> p m r u"))
-                else:
-                    nc.vector.tensor_copy(
-                        out=grouped[:, i], in_=xt[:].rearrange("p m u r -> p m r u")
+        def sort_words(b):
+            for m in range(ROW_TILES):
+                x_sorted[(b, m)] = sorted_pool.tile([P, BUNCH, HALVES, P], F32, name="x_sorted")
+                nc.vector.tensor_copy(
+                    out=x_sorted[(b, m)][:],
+                    in_=x_raw[(b, m)][:].bitcast(F32).rearrange("p (i q u) -> p i u q", q=P, u=HALVES),
+                )
+
+        def transpose(b):
+            for m in range(ROW_TILES):
+                grouped[(b, m)] = grouped_pool.tile(
+                    [P, BUNCH, P, HALVES], F32, name="grouped", align_bytes=64
+                )
+                for i0 in range(0, BUNCH, PER_BANK):
+                    xt = banks.tile([P, PER_BANK, HALVES, P], F32, name="xt", tag="bank")
+                    for j in range(PER_BANK):
+                        for u in range(HALVES):
+                            nc.tensor.transpose(
+                                out=xt[:, j, u, :],
+                                in_=x_sorted[(b, m)][:, i0 + j, u, :],
+                                identity=ident[:],
+                            )
+                    nc.scalar.copy(
+                        out=grouped[(b, m)][:, i0 : i0 + PER_BANK],
+                        in_=xt[:].rearrange("p j u r -> p j r u"),
                     )
-            for i in range(0, BUNCH, 2):
-                g = b * BUNCH + i
+
+        def quantise(b):
+            for m in range(ROW_TILES):
                 nc.vector.quantize_mx(
-                    out=x_codes[:, g : g + 2].rearrange("p g m r -> p (g m r)").bitcast(FP8X4),
-                    scales=x_planes[:, g : g + 2].rearrange("p g m r -> p (g m r)"),
-                    in_=grouped[:, i : i + 2].rearrange("p g m r u -> p (g m r u)").bitcast(BF16),
+                    out=x_codes[(b, m)][:].rearrange("p i r -> p (i r)").bitcast(FP8X4),
+                    scales=x_planes[(b, m)][:].rearrange("p i r -> p (i r)"),
+                    in_=grouped[(b, m)][:].rearrange("p i r u -> p (i r u)").bitcast(BF16),
                 )
 
         def multiply(w, b):
-            for g in range(b * BUNCH, (b + 1) * BUNCH):
-                for m in range(ROW_TILES):
+            for m in range(ROW_TILES):
+                for i in range(BUNCH):
+                    g = b * BUNCH + i
                     nc.tensor.matmul_mx(
                         out=acc[(w, m)][:],
-                        lhsT=x_codes[:, g, m, :].bitcast(FP8X4),
-                        lhsT_scale=x_planes[:, g, m, :],
-                        rhs=words[w][:, g, :].bitcast(FP4X4),
-                        rhs_scale=planes[w][:, g, :],
+                        lhsT=x_codes[(b, m)][:, i, :].bitcast(FP8X4),
+                        lhsT_scale=x_planes[(b, m)][:, i, :],
+                        rhs=words[(w, b)][:, i, :].bitcast(FP4X4),
+                        rhs_scale=planes[g // SCALE_RUN][:, g % SCALE_RUN, :],
                         start=(g == 0),
                         stop=(g == GROUPS - 1),
                     )
@@ -138,16 +163,20 @@ def tile_linearattention_pa_k_kernel(
         load_x(1)
         nc.sync.dma_start(out=bias_row[0:1, 0, :], in_=bk.unsqueeze(0))
         nc.sync.dma_start(out=bias_row[0:1, 1, :], in_=bv.unsqueeze(0))
+        sort_words(0)
         for b in range(BUNCHES):
-            load_words("k", Wk_words, b)
+            load_weight("k", b)
             if b + 2 < BUNCHES:
                 load_x(b + 2)
-            transpose_and_quantise(b)
+            if b + 1 < BUNCHES:
+                sort_words(b + 1)
+            transpose(b)
             if b > 0:
                 multiply("k", b - 1)
-        for b in range(BUNCHES):
-            load_words("v", Wv_words, b)
+            quantise(b)
         multiply("k", BUNCHES - 1)
+        for b in range(BUNCHES):
+            load_weight("v", b)
 
         for j in range(2):
             spread = banks.tile([P, H], F32, name="spread", tag="bank")

@@ -20,8 +20,10 @@ ROW_TILES = ROWS // P
 K_PASS = 4 * P
 GROUPS = D // K_PASS
 HALVES = 2
-BUNCH = 4
-BUNCHES = GROUPS // BUNCH
+SIZES = (2, 2) + (4,) * 7
+BUNCHES = len(SIZES)
+FIRST = tuple(sum(SIZES[:b]) for b in range(BUNCHES))
+AHEAD = 2
 PER_BANK = 2
 SCALE_RUN = GROUPS // 2
 
@@ -38,7 +40,7 @@ def tile_linearattention_pa_k_kernel(
 
     with ExitStack() as ctx:
         keep = ctx.enter_context(tc.tile_pool(name="keep", bufs=1))
-        x_pool = ctx.enter_context(tc.tile_pool(name="x_pool", bufs=6))
+        x_pool = ctx.enter_context(tc.tile_pool(name="x_pool", bufs=2 * (AHEAD + 1)))
         sorted_pool = ctx.enter_context(tc.tile_pool(name="sorted_pool", bufs=4))
         grouped_pool = ctx.enter_context(tc.tile_pool(name="grouped_pool", bufs=4))
         sums = ctx.enter_context(tc.psum_pool(name="sums", bufs=1))
@@ -49,7 +51,7 @@ def tile_linearattention_pa_k_kernel(
         for w in ("k", "v"):
             for b in range(BUNCHES):
                 words[(w, b)] = keep.tile(
-                    [P, BUNCH, 2 * H], U8, name="words_%s%d" % (w, b), align_bytes=64
+                    [P, SIZES[b], 2 * H], U8, name="words_%s%d" % (w, b), align_bytes=64
                 )
         planes = {}
         for run in range(GROUPS // SCALE_RUN):
@@ -59,10 +61,10 @@ def tile_linearattention_pa_k_kernel(
         for b in range(BUNCHES):
             for m in range(ROW_TILES):
                 x_codes[(b, m)] = keep.tile(
-                    [P, BUNCH, P], U32, name="x_codes%d_%d" % (b, m), align_bytes=64
+                    [P, SIZES[b], P], U32, name="x_codes%d_%d" % (b, m), align_bytes=64
                 )
                 x_planes[(b, m)] = keep.tile(
-                    [P, BUNCH, P], U8, name="x_planes%d_%d" % (b, m), align_bytes=64
+                    [P, SIZES[b], P], U8, name="x_planes%d_%d" % (b, m), align_bytes=64
                 )
         ident = keep.tile([P, P], F32, name="ident")
         ones = keep.tile([P, P], BF16, name="ones")
@@ -75,29 +77,30 @@ def tile_linearattention_pa_k_kernel(
             for m in range(ROW_TILES):
                 acc[(w, m)] = sums.tile([P, H], F32, name="acc_%s%d" % (w, m))
 
-        make_identity(nc, ident[:])
-        for run in range(GROUPS // SCALE_RUN):
-            nc.vector.memset(planes[run][:].bitcast(I32), 0)
         nc.vector.memset(bias_row[:].bitcast(I32), 0)
         nc.vector.memset(ones[:], 1.0)
-        nc.vector.memset(batch_of_row[:], 0.0)
+        make_identity(nc, ident[:])
+        nc.vector.memset(planes[0][:].bitcast(I32), 0)
+        for run in range(1, GROUPS // SCALE_RUN):
+            nc.gpsimd.memset(planes[run][:].bitcast(F32), 0.0)
+        nc.gpsimd.memset(batch_of_row[:], 0.0)
         for m in range(ROW_TILES):
             for half in range(P // SEQ):
                 c = m * (P // SEQ) + half
-                nc.vector.memset(batch_of_row[half * SEQ : (half + 1) * SEQ, m, c : c + 1], 1.0)
+                nc.gpsimd.memset(batch_of_row[half * SEQ : (half + 1) * SEQ, m, c : c + 1], 1.0)
 
         x_raw = {}
         x_sorted = {}
         grouped = {}
 
         def load_x(b):
-            cols = slice(b * BUNCH * K_PASS, (b + 1) * BUNCH * K_PASS)
+            cols = slice(FIRST[b] * K_PASS, (FIRST[b] + SIZES[b]) * K_PASS)
             for m in range(ROW_TILES):
-                x_raw[(b, m)] = x_pool.tile([P, BUNCH * K_PASS], BF16, name="x_raw")
+                x_raw[(b, m)] = x_pool.tile([P, SIZES[b] * K_PASS], BF16, name="x_raw")
                 nc.sync.dma_start(out=x_raw[(b, m)][:], in_=x_rows[m * P : (m + 1) * P, cols])
 
         def load_weight(w, b):
-            g0 = b * BUNCH
+            g0 = FIRST[b]
             if g0 % SCALE_RUN == 0:
                 by_row = scales_dram[w].rearrange("g q n -> q g n")
                 for r in range(4):
@@ -107,12 +110,12 @@ def tile_linearattention_pa_k_kernel(
                     )
             nc.sync.dma_start(
                 out=words[(w, b)][:].bitcast(I32),
-                in_=words_dram[w][g0 : g0 + BUNCH].rearrange("g p c -> p g c").bitcast(I32),
+                in_=words_dram[w][g0 : g0 + SIZES[b]].rearrange("g p c -> p g c").bitcast(I32),
             )
 
         def sort_words(b):
             for m in range(ROW_TILES):
-                x_sorted[(b, m)] = sorted_pool.tile([P, BUNCH, HALVES, P], F32, name="x_sorted")
+                x_sorted[(b, m)] = sorted_pool.tile([P, SIZES[b], HALVES, P], F32, name="x_sorted")
                 nc.vector.tensor_copy(
                     out=x_sorted[(b, m)][:],
                     in_=x_raw[(b, m)][:].bitcast(F32).rearrange("p (i q u) -> p i u q", q=P, u=HALVES),
@@ -121,11 +124,12 @@ def tile_linearattention_pa_k_kernel(
         def transpose(b):
             for m in range(ROW_TILES):
                 grouped[(b, m)] = grouped_pool.tile(
-                    [P, BUNCH, P, HALVES], F32, name="grouped", align_bytes=64
+                    [P, SIZES[b], P, HALVES], F32, name="grouped", align_bytes=64
                 )
-                for i0 in range(0, BUNCH, PER_BANK):
-                    xt = banks.tile([P, PER_BANK, HALVES, P], F32, name="xt", tag="bank")
-                    for j in range(PER_BANK):
+                for i0 in range(0, SIZES[b], PER_BANK):
+                    in_bank = min(PER_BANK, SIZES[b] - i0)
+                    xt = banks.tile([P, in_bank, HALVES, P], F32, name="xt", tag="bank")
+                    for j in range(in_bank):
                         for u in range(HALVES):
                             nc.tensor.transpose(
                                 out=xt[:, j, u, :],
@@ -133,7 +137,7 @@ def tile_linearattention_pa_k_kernel(
                                 identity=ident[:],
                             )
                     nc.scalar.copy(
-                        out=grouped[(b, m)][:, i0 : i0 + PER_BANK],
+                        out=grouped[(b, m)][:, i0 : i0 + in_bank],
                         in_=xt[:].rearrange("p j u r -> p j r u"),
                     )
 
@@ -145,10 +149,10 @@ def tile_linearattention_pa_k_kernel(
                     in_=grouped[(b, m)][:].rearrange("p i r u -> p (i r u)").bitcast(BF16),
                 )
 
-        def multiply(w, b):
-            for m in range(ROW_TILES):
-                for i in range(BUNCH):
-                    g = b * BUNCH + i
+        def multiply(w, b, row_tiles=range(ROW_TILES)):
+            for m in row_tiles:
+                for i in range(SIZES[b]):
+                    g = FIRST[b] + i
                     nc.tensor.matmul_mx(
                         out=acc[(w, m)][:],
                         lhsT=x_codes[(b, m)][:, i, :].bitcast(FP8X4),
@@ -159,29 +163,32 @@ def tile_linearattention_pa_k_kernel(
                         stop=(g == GROUPS - 1),
                     )
 
-        load_x(0)
-        load_x(1)
+        def spread_biases():
+            for j in range(2):
+                spread = banks.tile([P, H], F32, name="spread", tag="bank")
+                nc.tensor.matmul(out=spread[:], lhsT=ones[:], rhs=bias_row[:, j, :], start=True, stop=True)
+                nc.scalar.copy(out=bias_all[:, j, :], in_=spread[:])
+
         nc.sync.dma_start(out=bias_row[0:1, 0, :], in_=bk.unsqueeze(0))
         nc.sync.dma_start(out=bias_row[0:1, 1, :], in_=bv.unsqueeze(0))
+        for b in range(AHEAD):
+            load_x(b)
         sort_words(0)
         for b in range(BUNCHES):
             load_weight("k", b)
-            if b + 2 < BUNCHES:
-                load_x(b + 2)
+            if b + AHEAD < BUNCHES:
+                load_x(b + AHEAD)
             if b + 1 < BUNCHES:
                 sort_words(b + 1)
             transpose(b)
+            if b == 0:
+                spread_biases()
             if b > 0:
                 multiply("k", b - 1)
             quantise(b)
         multiply("k", BUNCHES - 1)
         for b in range(BUNCHES):
             load_weight("v", b)
-
-        for j in range(2):
-            spread = banks.tile([P, H], F32, name="spread", tag="bank")
-            nc.tensor.matmul(out=spread[:], lhsT=ones[:], rhs=bias_row[:, j, :], start=True, stop=True)
-            nc.scalar.copy(out=bias_all[:, j, :], in_=spread[:])
 
         feat = {}
         for m in range(ROW_TILES):

@@ -103,11 +103,13 @@ def tile_linearattention_pa_k_kernel(
             g0 = FIRST[b]
             if g0 % SCALE_RUN == 0:
                 by_row = scales_dram[w].rearrange("g q n -> q g n")
-                for r in range(4):
-                    nc.sync.dma_start(
-                        out=planes[g0 // SCALE_RUN][r : P : 32, :, :].bitcast(I32),
-                        in_=by_row[r : 16 : 4, g0 : g0 + SCALE_RUN, :].bitcast(I32),
-                    )
+                for part in range(0, SCALE_RUN, SCALE_RUN // 2):
+                    for q in range(8):
+                        p0 = 32 * (q // 4) + q % 4
+                        nc.sync.dma_start(
+                            out=planes[g0 // SCALE_RUN][p0 : P : 64, part : part + SCALE_RUN // 2, :].bitcast(I32),
+                            in_=by_row[q : 16 : 8, g0 + part : g0 + part + SCALE_RUN // 2, :].bitcast(I32),
+                        )
             nc.sync.dma_start(
                 out=words[(w, b)][:].bitcast(I32),
                 in_=words_dram[w][g0 : g0 + SIZES[b]].rearrange("g p c -> p g c").bitcast(I32),

@@ -103,13 +103,12 @@ def tile_linearattention_pa_k_kernel(
             g0 = FIRST[b]
             if g0 % SCALE_RUN == 0:
                 by_row = scales_dram[w].rearrange("g q n -> q g n")
-                for part in range(0, SCALE_RUN, SCALE_RUN // 2):
-                    for q in range(8):
-                        p0 = 32 * (q // 4) + q % 4
-                        nc.sync.dma_start(
-                            out=planes[g0 // SCALE_RUN][p0 : P : 64, part : part + SCALE_RUN // 2, :].bitcast(I32),
-                            in_=by_row[q : 16 : 8, g0 + part : g0 + part + SCALE_RUN // 2, :].bitcast(I32),
-                        )
+                for q in range(8):
+                    p0 = 32 * (q // 4) + q % 4
+                    nc.sync.dma_start(
+                        out=planes[g0 // SCALE_RUN][p0 : P : 64, :, :].bitcast(I32),
+                        in_=by_row[q : 16 : 8, g0 : g0 + SCALE_RUN, :].bitcast(I32),
+                    )
             nc.sync.dma_start(
                 out=words[(w, b)][:].bitcast(I32),
                 in_=words_dram[w][g0 : g0 + SIZES[b]].rearrange("g p c -> p g c").bitcast(I32),

@@ -12,6 +12,7 @@ FP8X4 = mybir.dt.float8_e4m3fn_x4
 FP4X4 = mybir.dt.float4_e2m1fn_x4
 ACT = mybir.ActivationFunctionType
 ALU = mybir.AluOpType
+AXIS = mybir.AxisListType
 
 P = 128
 BATCH, SEQ, D, H = 4, 64, 16384, 512
@@ -26,6 +27,9 @@ FIRST = tuple(sum(SIZES[:b]) for b in range(BUNCHES))
 AHEAD = 2
 PER_BANK = 2
 SCALE_RUN = GROUPS // 2
+H_TILES = H // P
+PER_TILE = P // SEQ
+SPLIT = 2
 
 FLOPS = 2 * ROWS * D * 2 * H
 
@@ -68,9 +72,15 @@ def tile_linearattention_pa_k_kernel(
                 )
         ident = keep.tile([P, P], F32, name="ident")
         ones = keep.tile([P, P], BF16, name="ones")
-        bias_row = keep.tile([P, 2, H], BF16, name="bias_row")
-        bias_all = keep.tile([P, 2, H], F32, name="bias_all")
-        batch_of_row = keep.tile([P, ROW_TILES, P], F32, name="batch_of_row")
+        bias_row = keep.tile([P, H], BF16, name="bias_row")
+        bias_all = keep.tile([P, H], F32, name="bias_all")
+        totals = {}
+        for j in range(2):
+            totals[j] = keep.tile([P, P], F32, name="totals%d" % j)
+        bv_rows = keep.tile([P, P], BF16, name="bv_rows")
+        ksum_rows = keep.tile([P, P], F32, name="ksum_rows")
+        bias_rows = keep.tile([P, P], F32, name="bias_rows")
+        kv_rows = keep.tile([P, P], F32, name="kv_rows")
 
         acc = {}
         for w in ("k", "v"):
@@ -83,11 +93,8 @@ def tile_linearattention_pa_k_kernel(
         nc.vector.memset(planes[0][:].bitcast(I32), 0)
         for run in range(1, GROUPS // SCALE_RUN):
             nc.gpsimd.memset(planes[run][:].bitcast(F32), 0.0)
-        nc.gpsimd.memset(batch_of_row[:], 0.0)
-        for m in range(ROW_TILES):
-            for half in range(P // SEQ):
-                c = m * (P // SEQ) + half
-                nc.gpsimd.memset(batch_of_row[half * SEQ : (half + 1) * SEQ, m, c : c + 1], 1.0)
+        for j in range(2):
+            nc.gpsimd.memset(totals[j][:], 0.0)
 
         x_raw = {}
         x_sorted = {}
@@ -164,16 +171,14 @@ def tile_linearattention_pa_k_kernel(
                         stop=(g == GROUPS - 1),
                     )
 
-        def spread_biases():
-            for j in range(2):
-                spread = banks.tile([P, H], F32, name="spread", tag="bank")
-                nc.tensor.matmul(out=spread[:], lhsT=ones[:], rhs=bias_row[:, j, :], start=True, stop=True)
-                nc.scalar.copy(out=bias_all[:, j, :], in_=spread[:])
+        def spread_bias():
+            spread = banks.tile([P, H], F32, name="spread", tag="bank")
+            nc.tensor.matmul(out=spread[:], lhsT=ones[:], rhs=bias_row[:], start=True, stop=True)
+            nc.scalar.copy(out=bias_all[:], in_=spread[:])
 
-        nc.sync.dma_start(out=bias_row[0:1, 0, :], in_=bk.unsqueeze(0))
-        nc.sync.dma_start(out=bias_row[0:1, 1, :], in_=bv.unsqueeze(0))
         for b in range(AHEAD):
             load_x(b)
+        nc.sync.dma_start(out=bias_row[0:1, :], in_=bk.unsqueeze(0))
         sort_words(0)
         for b in range(BUNCHES):
             load_weight("k", b)
@@ -183,18 +188,22 @@ def tile_linearattention_pa_k_kernel(
                 sort_words(b + 1)
             transpose(b)
             if b == 0:
-                spread_biases()
+                spread_bias()
             if b > 0:
                 multiply("k", b - 1)
             quantise(b)
         multiply("k", BUNCHES - 1)
         for b in range(BUNCHES):
             load_weight("v", b)
+        for n in range(BATCH):
+            nc.sync.dma_start(
+                out=bv_rows[n * H_TILES : (n + 1) * H_TILES, :], in_=bv.rearrange("(c l) -> c l", l=P)
+            )
 
         feat = {}
         for m in range(ROW_TILES):
             keyp = keep.tile([P, H], F32, name="keyp%d" % m)
-            nc.vector.tensor_tensor(out=keyp[:], in0=acc[("k", m)][:], in1=bias_all[:, 0, :], op=ALU.add)
+            nc.vector.tensor_tensor(out=keyp[:], in0=acc[("k", m)][:], in1=bias_all[:], op=ALU.add)
             below = keep.tile([P, H], F32, name="below%d" % m)
             nc.vector.tensor_scalar_min(out=below[:], in0=keyp[:], scalar1=0.0)
             nc.scalar.activation(out=below[:], in_=below[:], func=ACT.Exp)
@@ -203,29 +212,61 @@ def tile_linearattention_pa_k_kernel(
                 out=feat[m][:], in0=keyp[:], scalar=0.0, in1=below[:], op0=ALU.max, op1=ALU.add
             )
 
-        ksum = keep.tile([P, H], F32, name="ksum")
-        bias_part = keep.tile([P, H], F32, name="bias_part")
-        for b in range(BUNCHES):
+        def sum_rows(src, j, m, tiles):
+            turned = banks.tile([P, len(tiles), P], F32, name="turned", tag="bank")
+            for i, c in enumerate(tiles):
+                nc.tensor.transpose(out=turned[:, i, :], in_=src[:, c * P : (c + 1) * P], identity=ident[:])
+            first = m * PER_TILE * H_TILES
+            nc.vector.tensor_reduce(
+                out=totals[j][:, first : first + PER_TILE * H_TILES].rearrange("p (a c) -> p c a", a=PER_TILE)[
+                    :, tiles[0] : tiles[0] + len(tiles), :
+                ],
+                in_=turned[:].rearrange("p c (a s) -> p c a s", a=PER_TILE),
+                axis=AXIS.X,
+                op=ALU.add,
+            )
+
+        def turn_back(j):
+            back = banks.tile([P, P], F32, name="back", tag="bank")
+            nc.tensor.transpose(out=back[:], in_=totals[j][:], identity=ident[:])
+            return back
+
+        all_tiles = tuple(range(H_TILES))
+        out_rows = BATCH * H_TILES
+        prod = {}
+        for m in range(ROW_TILES):
+            prod[m] = keep.tile([P, H], F32, name="prod%d" % m)
+        for b in range(BUNCHES - SPLIT):
             multiply("v", b)
             if b == BUNCHES // 2:
-                ksum_ps = banks.tile([P, H], F32, name="ksum_ps", tag="bank")
                 for m in range(ROW_TILES):
-                    nc.tensor.matmul(
-                        out=ksum_ps[:], lhsT=batch_of_row[:, m, :], rhs=feat[m][:],
-                        start=(m == 0), stop=(m == ROW_TILES - 1),
-                    )
-                nc.vector.tensor_copy(out=ksum[:], in_=ksum_ps[:])
-                nc.vector.tensor_tensor(out=bias_part[:], in0=ksum[:], in1=bias_all[:, 1, :], op=ALU.mult)
-                nc.sync.dma_start(out=out_1, in_=ksum[0:BATCH, :])
-
-        kv_ps = banks.tile([P, H], F32, name="kv_ps", tag="bank")
-        for m in range(ROW_TILES):
-            prod = keep.tile([P, H], F32, name="prod%d" % m)
-            nc.vector.tensor_tensor(out=prod[:], in0=acc[("v", m)][:], in1=feat[m][:], op=ALU.mult)
-            nc.tensor.matmul(
-                out=kv_ps[:], lhsT=batch_of_row[:, m, :], rhs=prod[:],
-                start=(m == 0), stop=(m == ROW_TILES - 1),
+                    sum_rows(feat[m], 1, m, all_tiles)
+        for b in range(BUNCHES - SPLIT, BUNCHES):
+            multiply("v", b, (0,))
+        nc.vector.tensor_tensor(out=prod[0][:], in0=acc[("v", 0)][:], in1=feat[0][:], op=ALU.mult)
+        for b in range(BUNCHES - SPLIT, BUNCHES):
+            if b == BUNCHES - 1:
+                ksum_back = turn_back(1)
+                nc.scalar.copy(out=ksum_rows[0:out_rows, :], in_=ksum_back[0:out_rows, :])
+                nc.scalar.dma_start(
+                    out=out_1.rearrange("n (c l) -> (n c) l", l=P), in_=ksum_rows[0:out_rows, :]
+                )
+                sum_rows(prod[0], 0, 0, all_tiles)
+                nc.vector.tensor_tensor(
+                    out=bias_rows[0:out_rows, :], in0=ksum_rows[0:out_rows, :], in1=bv_rows[0:out_rows, :],
+                    op=ALU.mult,
+                )
+            multiply("v", b, (1,))
+        halves = (all_tiles[: H_TILES // 2], all_tiles[H_TILES // 2 :])
+        for tiles in halves:
+            cols = slice(tiles[0] * P, (tiles[-1] + 1) * P)
+            nc.vector.tensor_tensor(
+                out=prod[1][:, cols], in0=acc[("v", 1)][:, cols], in1=feat[1][:, cols], op=ALU.mult
             )
-        kv = keep.tile([P, H], F32, name="kv")
-        nc.vector.tensor_tensor(out=kv[:], in0=kv_ps[:], in1=bias_part[:], op=ALU.add)
-        nc.sync.dma_start(out=out_0, in_=kv[0:BATCH, :])
+        for tiles in halves:
+            sum_rows(prod[1], 0, 1, tiles)
+        kv_back = turn_back(0)
+        nc.vector.tensor_tensor(
+            out=kv_rows[0:out_rows, :], in0=kv_back[0:out_rows, :], in1=bias_rows[0:out_rows, :], op=ALU.add
+        )
+        nc.sync.dma_start(out=out_0.rearrange("n (c l) -> (n c) l", l=P), in_=kv_rows[0:out_rows, :])

@@ -26,7 +26,7 @@ BUNCHES = len(SIZES)
 FIRST = tuple(sum(SIZES[:b]) for b in range(BUNCHES))
 AHEAD = 2
 PER_BANK = 2
-SCALE_RUN = GROUPS // 2
+SCALE_RUN = GROUPS // 4
 H_TILES = H // P
 PER_TILE = P // SEQ
 SPLIT = 2
@@ -90,9 +90,11 @@ def tile_linearattention_pa_k_kernel(
         nc.vector.memset(bias_row[:].bitcast(I32), 0)
         nc.vector.memset(ones[:], 1.0)
         make_identity(nc, ident[:])
-        nc.vector.memset(planes[0][:].bitcast(I32), 0)
-        for run in range(1, GROUPS // SCALE_RUN):
-            nc.gpsimd.memset(planes[run][:].bitcast(F32), 0.0)
+        for run in range(GROUPS // SCALE_RUN):
+            if run < 2:
+                nc.vector.memset(planes[run][:].bitcast(I32), 0)
+            else:
+                nc.gpsimd.memset(planes[run][:].bitcast(F32), 0.0)
         for j in range(2):
             nc.gpsimd.memset(totals[j][:], 0.0)
 

@@ -102,26 +102,43 @@ def tile_linearattention_pa_k_kernel(
         x_sorted = {}
         grouped = {}
 
-        def load_x(b):
+        runs = [(w, run) for w in ("k", "v") for run in range(GROUPS // SCALE_RUN)]
+        asked = {}
+
+        def load_scale_rows(w, run, count):
+            by_row = scales_dram[w].rearrange("g q n -> q g n")
+            g0 = run * SCALE_RUN
+            started = asked.get((w, run), 0)
+            asked[(w, run)] = min(started + count, 8)
+            for q in range(started, asked[(w, run)]):
+                p0 = 32 * (q // 4) + q % 4
+                nc.sync.dma_start(
+                    out=planes[run][p0 : P : 64, :, :].bitcast(I32),
+                    in_=by_row[q : 16 : 8, g0 : g0 + SCALE_RUN, :].bitcast(I32),
+                )
+
+        def weave(w, b, count):
+            run = FIRST[b] // SCALE_RUN
+            following = runs.index((w, run)) + 1
+            if following < len(runs) and b in [c for c in range(BUNCHES) if FIRST[c] // SCALE_RUN == run][-2:]:
+                load_scale_rows(runs[following][0], runs[following][1], count)
+
+        def load_x(b, with_bunch=None):
             cols = slice(FIRST[b] * K_PASS, (FIRST[b] + SIZES[b]) * K_PASS)
             for m in range(ROW_TILES):
                 x_raw[(b, m)] = x_pool.tile([P, SIZES[b] * K_PASS], BF16, name="x_raw")
                 nc.sync.dma_start(out=x_raw[(b, m)][:], in_=x_rows[m * P : (m + 1) * P, cols])
+                if with_bunch is not None:
+                    weave("k", with_bunch, 1)
 
         def load_weight(w, b):
             g0 = FIRST[b]
-            if g0 % SCALE_RUN == 0:
-                by_row = scales_dram[w].rearrange("g q n -> q g n")
-                for q in range(8):
-                    p0 = 32 * (q // 4) + q % 4
-                    nc.sync.dma_start(
-                        out=planes[g0 // SCALE_RUN][p0 : P : 64, :, :].bitcast(I32),
-                        in_=by_row[q : 16 : 8, g0 : g0 + SCALE_RUN, :].bitcast(I32),
-                    )
+            load_scale_rows(w, g0 // SCALE_RUN, 8)
             nc.sync.dma_start(
                 out=words[(w, b)][:].bitcast(I32),
                 in_=words_dram[w][g0 : g0 + SIZES[b]].rearrange("g p c -> p g c").bitcast(I32),
             )
+            weave(w, b, 2)
 
         def sort_words(b):
             for m in range(ROW_TILES):
@@ -185,7 +202,7 @@ def tile_linearattention_pa_k_kernel(
         for b in range(BUNCHES):
             load_weight("k", b)
             if b + AHEAD < BUNCHES:
-                load_x(b + AHEAD)
+                load_x(b + AHEAD, b)
             if b + 1 < BUNCHES:
                 sort_words(b + 1)
             transpose(b)

from contextlib import ExitStack

import concourse.mybir as mybir
from concourse.masks import make_identity

F32 = mybir.dt.float32
BF16 = mybir.dt.bfloat16
I32 = mybir.dt.int32
U32 = mybir.dt.uint32
U8 = mybir.dt.uint8
FP8X4 = mybir.dt.float8_e4m3fn_x4
FP4X4 = mybir.dt.float4_e2m1fn_x4
ACT = mybir.ActivationFunctionType
ALU = mybir.AluOpType
AXIS = mybir.AxisListType

P = 128
BATCH, SEQ, D, H = 4, 64, 16384, 512
ROWS = BATCH * SEQ
ROW_TILES = ROWS // P
K_PASS = 4 * P
GROUPS = D // K_PASS
HALVES = 2
SIZES = (2, 2) + (4,) * 7
BUNCHES = len(SIZES)
FIRST = tuple(sum(SIZES[:b]) for b in range(BUNCHES))
AHEAD = 2
PER_BANK = 2
SCALE_RUN = GROUPS // 4
H_TILES = H // P
PER_TILE = P // SEQ
SPLIT = 2

FLOPS = 2 * ROWS * D * 2 * H


def tile_linearattention_pa_k_kernel(
    tc, x, Wk_words, Wk_scales, bk, Wv_words, Wv_scales, bv, out_0, out_1
):
    nc = tc.nc
    x_rows = x.rearrange("n s d -> (n s) d")
    words_dram = {"k": Wk_words, "v": Wv_words}
    scales_dram = {"k": Wk_scales, "v": Wv_scales}

    with ExitStack() as ctx:
        keep = ctx.enter_context(tc.tile_pool(name="keep", bufs=1))
        x_pool = ctx.enter_context(tc.tile_pool(name="x_pool", bufs=2 * (AHEAD + 1)))
        sorted_pool = ctx.enter_context(tc.tile_pool(name="sorted_pool", bufs=4))
        grouped_pool = ctx.enter_context(tc.tile_pool(name="grouped_pool", bufs=4))
        sums = ctx.enter_context(tc.psum_pool(name="sums", bufs=1))
        banks = ctx.enter_context(tc.psum_pool(name="banks", bufs=4))
        ctx.enter_context(tc.manual_schedule())

        words = {}
        for w in ("k", "v"):
            for b in range(BUNCHES):
                words[(w, b)] = keep.tile(
                    [P, SIZES[b], 2 * H], U8, name="words_%s%d" % (w, b), align_bytes=64
                )
        planes = {}
        for run in range(GROUPS // SCALE_RUN):
            planes[run] = keep.tile([P, SCALE_RUN, H], U8, name="planes%d" % run, align_bytes=64)
        x_codes = {}
        x_planes = {}
        for b in range(BUNCHES):
            for m in range(ROW_TILES):
                x_codes[(b, m)] = keep.tile(
                    [P, SIZES[b], P], U32, name="x_codes%d_%d" % (b, m), align_bytes=64
                )
                x_planes[(b, m)] = keep.tile(
                    [P, SIZES[b], P], U8, name="x_planes%d_%d" % (b, m), align_bytes=64
                )
        ident = keep.tile([P, P], F32, name="ident")
        ones = keep.tile([P, P], BF16, name="ones")
        bias_row = keep.tile([P, H], BF16, name="bias_row")
        bias_all = keep.tile([P, H], F32, name="bias_all")
        totals = {}
        for j in range(2):
            totals[j] = keep.tile([P, P], F32, name="totals%d" % j)
        bv_rows = keep.tile([P, P], BF16, name="bv_rows")
        ksum_rows = keep.tile([P, P], F32, name="ksum_rows")
        bias_rows = keep.tile([P, P], F32, name="bias_rows")
        kv_rows = keep.tile([P, P], F32, name="kv_rows")

        acc = {}
        for w in ("k", "v"):
            for m in range(ROW_TILES):
                acc[(w, m)] = sums.tile([P, H], F32, name="acc_%s%d" % (w, m))

        nc.vector.memset(bias_row[:].bitcast(I32), 0)
        nc.vector.memset(ones[:], 1.0)
        make_identity(nc, ident[:])
        for run in range(GROUPS // SCALE_RUN):
            if run < 2:
                nc.vector.memset(planes[run][:].bitcast(I32), 0)
            else:
                nc.gpsimd.memset(planes[run][:].bitcast(F32), 0.0)
        for j in range(2):
            nc.gpsimd.memset(totals[j][:], 0.0)

        x_raw = {}
        x_sorted = {}
        grouped = {}

        runs = [(w, run) for w in ("k", "v") for run in range(GROUPS // SCALE_RUN)]
        asked = {}

        def load_scale_rows(w, run, count):
            by_row = scales_dram[w].rearrange("g q n -> q g n")
            g0 = run * SCALE_RUN
            started = asked.get((w, run), 0)
            asked[(w, run)] = min(started + count, 8)
            for q in range(started, asked[(w, run)]):
                p0 = 32 * (q // 4) + q % 4
                nc.sync.dma_start(
                    out=planes[run][p0 : P : 64, :, :].bitcast(I32),
                    in_=by_row[q : 16 : 8, g0 : g0 + SCALE_RUN, :].bitcast(I32),
                )

        def weave(w, b, count):
            run = FIRST[b] // SCALE_RUN
            following = runs.index((w, run)) + 1
            if following < len(runs) and b in [c for c in range(BUNCHES) if FIRST[c] // SCALE_RUN == run][-2:]:
                load_scale_rows(runs[following][0], runs[following][1], count)

        def load_x(b, with_bunch=None):
            cols = slice(FIRST[b] * K_PASS, (FIRST[b] + SIZES[b]) * K_PASS)
            for m in range(ROW_TILES):
                x_raw[(b, m)] = x_pool.tile([P, SIZES[b] * K_PASS], BF16, name="x_raw")
                nc.sync.dma_start(out=x_raw[(b, m)][:], in_=x_rows[m * P : (m + 1) * P, cols])
                if with_bunch is not None:
                    weave("k", with_bunch, 1)

        def load_weight(w, b):
            g0 = FIRST[b]
            load_scale_rows(w, g0 // SCALE_RUN, 8)
            nc.sync.dma_start(
                out=words[(w, b)][:].bitcast(I32),
                in_=words_dram[w][g0 : g0 + SIZES[b]].rearrange("g p c -> p g c").bitcast(I32),
            )
            weave(w, b, 2)

        def sort_words(b):
            for m in range(ROW_TILES):
                x_sorted[(b, m)] = sorted_pool.tile([P, SIZES[b], HALVES, P], F32, name="x_sorted")
                nc.vector.tensor_copy(
                    out=x_sorted[(b, m)][:],
                    in_=x_raw[(b, m)][:].bitcast(F32).rearrange("p (i q u) -> p i u q", q=P, u=HALVES),
                )

        def transpose(b):
            for m in range(ROW_TILES):
                grouped[(b, m)] = grouped_pool.tile(
                    [P, SIZES[b], P, HALVES], F32, name="grouped", align_bytes=64
                )
                for i0 in range(0, SIZES[b], PER_BANK):
                    in_bank = min(PER_BANK, SIZES[b] - i0)
                    xt = banks.tile([P, in_bank, HALVES, P], F32, name="xt", tag="bank")
                    for j in range(in_bank):
                        for u in range(HALVES):
                            nc.tensor.transpose(
                                out=xt[:, j, u, :],
                                in_=x_sorted[(b, m)][:, i0 + j, u, :],
                                identity=ident[:],
                            )
                    nc.scalar.copy(
                        out=grouped[(b, m)][:, i0 : i0 + in_bank],
                        in_=xt[:].rearrange("p j u r -> p j r u"),
                    )

        def quantise(b):
            for m in range(ROW_TILES):
                nc.vector.quantize_mx(
                    out=x_codes[(b, m)][:].rearrange("p i r -> p (i r)").bitcast(FP8X4),
                    scales=x_planes[(b, m)][:].rearrange("p i r -> p (i r)"),
                    in_=grouped[(b, m)][:].rearrange("p i r u -> p (i r u)").bitcast(BF16),
                )

        def multiply(w, b, row_tiles=range(ROW_TILES)):
            for m in row_tiles:
                for i in range(SIZES[b]):
                    g = FIRST[b] + i
                    nc.tensor.matmul_mx(
                        out=acc[(w, m)][:],
                        lhsT=x_codes[(b, m)][:, i, :].bitcast(FP8X4),
                        lhsT_scale=x_planes[(b, m)][:, i, :],
                        rhs=words[(w, b)][:, i, :].bitcast(FP4X4),
                        rhs_scale=planes[g // SCALE_RUN][:, g % SCALE_RUN, :],
                        start=(g == 0),
                        stop=(g == GROUPS - 1),
                    )

        def spread_bias():
            spread = banks.tile([P, H], F32, name="spread", tag="bank")
            nc.tensor.matmul(out=spread[:], lhsT=ones[:], rhs=bias_row[:], start=True, stop=True)
            nc.scalar.copy(out=bias_all[:], in_=spread[:])

        for b in range(AHEAD):
            load_x(b)
        nc.sync.dma_start(out=bias_row[0:1, :], in_=bk.unsqueeze(0))
        sort_words(0)
        for b in range(BUNCHES):
            load_weight("k", b)
            if b + AHEAD < BUNCHES:
                load_x(b + AHEAD, b)
            if b + 1 < BUNCHES:
                sort_words(b + 1)
            transpose(b)
            if b == 0:
                spread_bias()
            if b > 0:
                multiply("k", b - 1)
            quantise(b)
        multiply("k", BUNCHES - 1)
        for b in range(BUNCHES):
            load_weight("v", b)
        for n in range(BATCH):
            nc.sync.dma_start(
                out=bv_rows[n * H_TILES : (n + 1) * H_TILES, :], in_=bv.rearrange("(c l) -> c l", l=P)
            )

        feat = {}
        for m in range(ROW_TILES):
            keyp = keep.tile([P, H], F32, name="keyp%d" % m)
            nc.vector.tensor_tensor(out=keyp[:], in0=acc[("k", m)][:], in1=bias_all[:], op=ALU.add)
            below = keep.tile([P, H], F32, name="below%d" % m)
            nc.vector.tensor_scalar_min(out=below[:], in0=keyp[:], scalar1=0.0)
            nc.scalar.activation(out=below[:], in_=below[:], func=ACT.Exp)
            feat[m] = keep.tile([P, H], F32, name="feat%d" % m)
            nc.vector.scalar_tensor_tensor(
                out=feat[m][:], in0=keyp[:], scalar=0.0, in1=below[:], op0=ALU.max, op1=ALU.add
            )

        def sum_rows(src, j, m, tiles):
            turned = banks.tile([P, len(tiles), P], F32, name="turned", tag="bank")
            for i, c in enumerate(tiles):
                nc.tensor.transpose(out=turned[:, i, :], in_=src[:, c * P : (c + 1) * P], identity=ident[:])
            first = m * PER_TILE * H_TILES
            nc.vector.tensor_reduce(
                out=totals[j][:, first : first + PER_TILE * H_TILES].rearrange("p (a c) -> p c a", a=PER_TILE)[
                    :, tiles[0] : tiles[0] + len(tiles), :
                ],
                in_=turned[:].rearrange("p c (a s) -> p c a s", a=PER_TILE),
                axis=AXIS.X,
                op=ALU.add,
            )

        def turn_back(j):
            back = banks.tile([P, P], F32, name="back", tag="bank")
            nc.tensor.transpose(out=back[:], in_=totals[j][:], identity=ident[:])
            return back

        all_tiles = tuple(range(H_TILES))
        out_rows = BATCH * H_TILES
        prod = {}
        for m in range(ROW_TILES):
            prod[m] = keep.tile([P, H], F32, name="prod%d" % m)
        for b in range(BUNCHES - SPLIT):
            multiply("v", b)
            if b == BUNCHES // 2:
                for m in range(ROW_TILES):
                    sum_rows(feat[m], 1, m, all_tiles)
        for b in range(BUNCHES - SPLIT, BUNCHES):
            multiply("v", b, (0,))
        nc.vector.tensor_tensor(out=prod[0][:], in0=acc[("v", 0)][:], in1=feat[0][:], op=ALU.mult)
        for b in range(BUNCHES - SPLIT, BUNCHES):
            if b == BUNCHES - 1:
                ksum_back = turn_back(1)
                nc.scalar.copy(out=ksum_rows[0:out_rows, :], in_=ksum_back[0:out_rows, :])
                nc.scalar.dma_start(
                    out=out_1.rearrange("n (c l) -> (n c) l", l=P), in_=ksum_rows[0:out_rows, :]
                )
                sum_rows(prod[0], 0, 0, all_tiles)
                nc.vector.tensor_tensor(
                    out=bias_rows[0:out_rows, :], in0=ksum_rows[0:out_rows, :], in1=bv_rows[0:out_rows, :],
                    op=ALU.mult,
                )
            multiply("v", b, (1,))
        halves = (all_tiles[: H_TILES // 2], all_tiles[H_TILES // 2 :])
        for tiles in halves:
            cols = slice(tiles[0] * P, (tiles[-1] + 1) * P)
            nc.vector.tensor_tensor(
                out=prod[1][:, cols], in0=acc[("v", 1)][:, cols], in1=feat[1][:, cols], op=ALU.mult
            )
        for tiles in halves:
            sum_rows(prod[1], 0, 1, tiles)
        kv_back = turn_back(0)
        nc.vector.tensor_tensor(
            out=kv_rows[0:out_rows, :], in0=kv_back[0:out_rows, :], in1=bias_rows[0:out_rows, :], op=ALU.add
        )
        nc.sync.dma_start(out=out_0.rearrange("n (c l) -> (n c) l", l=P), in_=kv_rows[0:out_rows, :])
